import numpy as np
import ml_dtypes


def mxq(x, axis, fmt="e4m3"):
    dtype, down = {"e4m3": (ml_dtypes.float8_e4m3fn, 7), "e5m2": (ml_dtypes.float8_e5m2, 14)}[fmt]
    v = np.moveaxis(np.asarray(x, np.float32).astype(ml_dtypes.bfloat16).astype(np.float64), axis, -1)
    blocks = v.reshape(v.shape[:-1] + (-1, 32))
    amax = np.abs(blocks).max(-1, keepdims=True)
    byte = np.maximum(np.where(amax > 0, np.frexp(amax)[1] - 1 + 127, 0) - down, 1)
    scale = np.exp2(byte - 127.0)
    codes = (blocks / scale).astype(np.float32).astype(dtype).astype(np.float64)
    return np.moveaxis((codes * scale).reshape(v.shape), -1, axis)


WIDE = False


def mx_kscale(k):
    if not WIDE:
        return np.ones(k)
    levels = np.array([10, -10, 5, -5, 0])
    if k % 512:
        return np.exp2(np.random.permutation(np.resize(levels, k // 32))).repeat(32)
    a = np.empty((k // 512, 16))
    for p in range(k // 512):
        a[p, :8] = np.random.permutation(np.resize(levels, 8))
        for g in range(8):
            far = levels[np.abs(levels - a[p, g]) >= 10]
            a[p, g + 8] = far[np.random.randint(len(far))]
    return np.exp2(a.ravel()).repeat(32)


BF16 = ml_dtypes.bfloat16


def bf(x):
    return np.asarray(x, np.float32).astype(BF16)


def f64(x):
    return np.asarray(x).astype(np.float64)


N, D, H, E = 1024, 512, 2048, 8

CLAMP_MAX = float(np.log(100.0))


def setup_inputs():
    s, t = mx_kscale(D), mx_kscale(H)
    return {"x": bf(np.random.standard_normal((N, D)) * s),
            "W1": bf(np.random.standard_normal((E, D, H)) / np.sqrt(D) / s[:, None] * t),
            "b1": bf(np.random.standard_normal((E, H)) * 0.1 * t),
            "W2": bf(np.random.standard_normal((E, H, D)) / np.sqrt(H) / t[:, None]),
            "b2": bf(np.random.standard_normal((E, D)) * 0.1),
            "temperature": bf(np.log(2.0) + 0.1 * np.random.standard_normal((1,)))}


def reference(x, W1, b1, W2, b2, temperature):
    xe = f64(x).reshape(E, N // E, D)
    h = np.maximum((mxq(xe, 2, "e4m3") @ mxq(f64(W1), 1, "e4m3")) + f64(b1)[:, None, :], 0.0)
    y = (mxq(h, 2, "e4m3") @ mxq(f64(W2), 1, "e4m3")) + f64(b2)[:, None, :]
    logit_scale = np.exp(np.minimum(f64(temperature), CLAMP_MAX))
    return y.reshape(N, D) * logit_scale

@@ -1,0 +1,375 @@
+import math
+from contextlib import ExitStack
+
+import concourse.mybir as mybir
+from concourse.masks import make_identity
+
+FP8X4 = mybir.dt.float8_e4m3fn_x4
+BF16 = mybir.dt.bfloat16
+F32 = mybir.dt.float32
+U32 = mybir.dt.uint32
+U8 = mybir.dt.uint8
+ACT = mybir.ActivationFunctionType
+ALU = mybir.AluOpType
+
+P = 128
+N_TOK, D, H = 1024, 512, 2048
+FLOPS = 2 * N_TOK * D * H * 2
+CLAMP_MAX = math.log(100.0)
+ORDER = "four"
+PINNED = True
+
+E = 8
+RAW_BUFS = 5
+
+
+V_EXTRA = (7,)
+S_EXTRA = ()
+
+
+def make_plan(tail_swap=True, v_extra=V_EXTRA, s_extra=S_EXTRA):
+    seq = []
+    for e in range(E):
+        seq.append(("W1", e))
+        seq.append(("W2", e))
+    if tail_swap:
+        seq[13], seq[14] = seq[14], seq[13]
+    where = dict((m, i) for i, m in enumerate(seq))
+    n = len(seq)
+    ops = []
+    q_done = [[] for unused in range(n)]
+    z_wait = []
+    z_done = [0] * E
+    hreg_wait = []
+    hq_wait = []
+    y_wait = []
+    hq_done = []
+    taken = [0, 0, 0, 0]
+    hold = [False]
+    passes = [[] for unused in range(E)]
+
+    def try_mm2():
+        if hold[0]:
+            return
+        for e in range(E):
+            if e in hq_done:
+                for c in q_done[where[("W2", e)]]:
+                    if c not in passes[e]:
+                        passes[e].append(c)
+                        ops.append(("mm2", e, c, len(passes[e]) == 1, len(passes[e]) == 4))
+                        if len(passes[e]) == 4:
+                            y_wait.append(e)
+
+    def q(i, c0, c1):
+        ops.append(("q", i, c0, c1))
+        kind, e = seq[i]
+        for c in range(c0, c1):
+            q_done[i].append(c)
+            if kind == "W1":
+                ops.append(("mm1", e, c))
+                z_wait.append((e, c))
+        try_mm2()
+
+    def z_slot():
+        while taken[0] < len(z_wait):
+            e, g = z_wait[taken[0]]
+            taken[0] += 1
+            ops.append(("zout", e, g))
+            z_done[e] += 1
+            if z_done[e] == 4:
+                hreg_wait.append(e)
+
+    def y_slot(limit):
+        while taken[1] < limit:
+            e = y_wait[taken[1]]
+            taken[1] += 1
+            ops.append(("yout", e))
+            ops.append(("st", e))
+
+    def hreg_slot(limit):
+        while taken[2] < limit:
+            e = hreg_wait[taken[2]]
+            taken[2] += 1
+            ops.append(("hreg", e))
+            hq_wait.append(e)
+
+    def hq_slot():
+        while taken[3] < len(hq_wait):
+            e = hq_wait[taken[3]]
+            taken[3] += 1
+            ops.append(("hq", e))
+            hq_done.append(e)
+            try_mm2()
+
+    ops.append(("ldsmall",))
+    ops.append(("ld", 0, 0, 1))
+    ops.append(("ld", 0, 1, 2))
+    ops.append(("ldx", 0, 2))
+    ops.append(("ld", 0, 2, 3))
+    ops.append(("ld", 0, 3, 4))
+    for i in range(1, RAW_BUFS):
+        ops.append(("ld", i, 0, 2))
+        if i == 2:
+            ops.append(("ldx", 2, 4))
+        ops.append(("ld", i, 2, 4))
+    b2 = [0, 0]
+    for i in range(n + 1):
+        last = i >= n - 1
+        h_ready = len(hreg_wait)
+        y_ready = len(y_wait)
+        hold[0] = not last
+        if i >= 3 and b2[0] < E and (i % 2 == 1 or i == n - 2):
+            ops.append(("b2s", b2[0]))
+            b2[0] += 1
+        if i >= 2 and b2[1] < E and (i % 2 == 0 or i == n - 3):
+            ops.append(("b2p", b2[1]))
+            b2[1] += 1
+        if i in (2, 6, 10):
+            ops.append(("xtp", i // 2 + 1, i // 2 + 3))
+        if i < n:
+            ops.append(("cp", "S", i, 1, 2))
+            ops.append(("cp", "V", i, 0, 1))
+        if i == 0:
+            ops.append(("consts",))
+            ops.append(("exp",))
+            ops.append(("xtp", 0, 2))
+            ops.append(("xcp", 0, 2))
+        if i < n:
+            ops.append(("cp", "S" if i in s_extra else "V", i, 2, 3))
+            ops.append(("cp", "V" if i in v_extra else "S", i, 3, 4))
+            if i in (1, 5):
+                ops.append(("ldx", (i + 7) // 2, (i + 7) // 2 + 2))
+            if i + RAW_BUFS < n:
+                ops.append(("ld", i + RAW_BUFS, 0, 2))
+                ops.append(("ld", i + RAW_BUFS, 2, 4))
+        hreg_slot(h_ready)
+        if i == 0:
+            ops.append(("b1T",))
+            ops.append(("xq", 0, 2))
+        if i in (3, 7, 11):
+            ops.append(("xcp", (i + 1) // 2, (i + 1) // 2 + 2))
+        if i > 0:
+            q(i - 1, 3, 4)
+        z_slot()
+        hold[0] = False
+        try_mm2()
+        hold[0] = not last
+        if i in (4, 8, 12):
+            ops.append(("xq", i // 2, i // 2 + 2))
+        if i < n:
+            q(i, 0, 1)
+            q(i, 2, 3)
+        hq_slot()
+        if i < n:
+            q(i, 1, 2)
+        y_slot(y_ready)
+    hold[0] = False
+    hreg_slot(len(hreg_wait))
+    hq_slot()
+    y_slot(len(y_wait))
+    return seq, ops
+
+
+def tile_moelayer_kernel(tc, x, W1, b1, W2, b2, temperature, out):
+    nc = tc.nc
+    seq, ops = make_plan()
+    with ExitStack() as ctx:
+        const = ctx.enter_context(tc.tile_pool(name="const", bufs=1))
+        rawp = ctx.enter_context(tc.tile_pool(name="raw", bufs=RAW_BUFS))
+        gvp = ctx.enter_context(tc.tile_pool(name="gvp", bufs=3))
+        gsp = ctx.enter_context(tc.tile_pool(name="gsp", bufs=4))
+        codes = ctx.enter_context(tc.tile_pool(name="codes", bufs=2))
+        hp = ctx.enter_context(tc.tile_pool(name="hp", bufs=2))
+        outp = ctx.enter_context(tc.tile_pool(name="outp", bufs=3))
+        b2sp = ctx.enter_context(tc.tile_pool(name="b2sp", bufs=2))
+        zp = ctx.enter_context(tc.psum_pool(name="zp", bufs=6))
+        yp = ctx.enter_context(tc.psum_pool(name="yp", bufs=2))
+        if PINNED:
+            ctx.enter_context(tc.manual_schedule())
+
+        raw = {}
+        grouped = {}
+        wc = {}
+        ws = {}
+        zt = {}
+        hT = {}
+        hg = {}
+        hc = {}
+        hs = {}
+        yt = {}
+        ot = {}
+        held = {}
+        pb = {}
+        bs = {}
+
+        x_sb = const.tile([P, E, D], BF16, name="x_sb")
+        xg = const.tile([P, E * P * 4], BF16, name="xg", align_bytes=64)
+        xc = const.tile([P, E * P], U32, name="xc", align_bytes=64)
+        xs = const.tile([P, E * P], U8, name="xs", align_bytes=64)
+        x_words = x_sb[:].bitcast(F32).rearrange("p e (v u) -> p e u v", u=2)
+        xg_words = xg[:].bitcast(F32).rearrange("p (e r u) -> p e r u", e=E, u=2)
+        x_view = x.rearrange("(e r) d -> r e d", e=E)
+        t_sb = const.tile([P, 1], BF16, name="t_sb")
+        t_min = const.tile([P, 1], F32, name="t_min")
+        s_col = const.tile([P, 1], F32, name="s_col")
+        b1_raw = const.tile([P, 512], BF16, name="b1_raw")
+        b1_g = const.tile([P, 4, P], BF16, name="b1_g")
+        b1T = const.tile([P, 4, 32], F32, name="b1T")
+        warm = const.tile([P, 2], F32, name="warm")
+        b2row = const.tile([P, E * D], BF16, name="b2row")
+        ones = const.tile([P, P], BF16, name="ones")
+        ident_f = const.tile([P, P], F32, name="ident_f")
+        ident_b = const.tile([P, P], BF16, name="ident_b")
+
+        for op in ops:
+            kind = op[0]
+            if kind == "ldsmall":
+                nc.vector.memset(warm[:], 0.0)
+                nc.vector.memset(b1_raw[:], 0.0)
+                nc.scalar.dma_start(out=t_sb[:], in_=temperature.partition_broadcast(P))
+                nc.scalar.dma_start(out=b1_raw[0:32, :], in_=b1.rearrange("e (g f) -> (e g) f", g=4))
+                nc.scalar.activation(out=warm[:, 1:2], in_=warm[:, 0:1], func=ACT.Exp)
+                make_identity(nc, ident_f[:])
+                make_identity(nc, ident_b[:])
+                nc.gpsimd.memset(b2row[:].bitcast(F32), 0.0)
+                nc.gpsimd.memset(ones[:], 1.0)
+                nc.gpsimd.dma_start(out=b2row[0:1, :], in_=b2.rearrange("(o e) d -> o (e d)", o=1))
+            elif kind == "ld":
+                i, a, b = op[1], op[2], op[3]
+                mk, e = seq[i]
+                if i not in raw:
+                    raw[i] = rawp.tile([P, 4, 4, 512], BF16, name="raw_%d" % i, tag="raw")
+                if mk == "W1":
+                    dst = raw[i][:].rearrange("p j g w -> p j (g w)")
+                    src = W1[e].rearrange("(p j) w -> p j w", j=4)
+                    nc.sync.dma_start(out=dst[:, :, 512 * a:512 * b], in_=src[:, :, 512 * a:512 * b])
+                else:
+                    if ORDER == "pair":
+                        src = W2[e].rearrange("(a p k) d -> p a (k d)", p=P, k=2)
+                        dst = raw[i][:].rearrange("p g (u k) d -> p (g u) (k d)", u=2)
+                        nc.sync.dma_start(out=dst[:, 2 * a:2 * b, :], in_=src[:, 2 * a:2 * b, :])
+                    else:
+                        src = W2[e].rearrange("(g p t) d -> p g (t d)", p=P, t=4)
+                        dst = raw[i][:].rearrange("p g t d -> p g (t d)")
+                        nc.sync.dma_start(out=dst[:, a:b, :], in_=src[:, a:b, :])
+            elif kind == "ldx":
+                a, b = op[1], op[2]
+                nc.sync.dma_start(out=x_sb[:, a:b, :], in_=x_view[:, a:b, :])
+            elif kind == "consts":
+                nc.vector.tensor_scalar_min(out=t_min[:], in0=t_sb[:], scalar1=CLAMP_MAX)
+                if ORDER == "pair":
+                    nc.vector.tensor_copy(out=b1_g[:].rearrange("p (u k) m -> p u k m", u=2),
+                                          in_=b1_raw[:].rearrange("p (u m k) -> p u k m", u=2, k=2))
+                else:
+                    nc.vector.tensor_copy(out=b1_g[:], in_=b1_raw[:].rearrange("p (m t) -> p t m", t=4))
+                b1_ps = zp.tile([P, 4, P], BF16, name="b1_ps", tag="z")
+                for t in range(4):
+                    nc.tensor.transpose(b1_ps[:, t, :], b1_g[:, t, :], ident_b[:])
+                held["b1_ps"] = b1_ps
+            elif kind == "b1T":
+                nc.vector.tensor_copy(out=b1T[:], in_=held["b1_ps"][:, :, 0:32])
+            elif kind == "exp":
+                nc.scalar.activation(out=s_col[:], in_=t_min[:], func=ACT.Exp)
+            elif kind == "xtp":
+                pair = op[1] // 2
+                xt = zp.tile([P, 4, P], F32, name="xt", tag="z")
+                held[("xt", pair)] = xt
+                for a in range(2):
+                    for u in range(2):
+                        nc.tensor.transpose(xt[:, 2 * a + u, :], x_words[:, 2 * pair + a, u, :], ident_f[:])
+            elif kind == "xcp":
+                pair = op[1] // 2
+                nc.scalar.copy(out=xg_words[:, 2 * pair:2 * pair + 2, :, :],
+                               in_=held[("xt", pair)][:].rearrange("p (a u) r -> p a r u", u=2))
+            elif kind == "xq":
+                a, b = op[1], op[2]
+                nc.vector.quantize_mx(out=xc[:, P * a:P * b].bitcast(FP8X4), scales=xs[:, P * a:P * b],
+                                      in_=xg[:, 4 * P * a:4 * P * b])
+            elif kind == "cp":
+                eng, i, c = op[1], op[2], op[3]
+                mk, e = seq[i]
+                if eng == "V":
+                    g = gvp.tile([P, 2048], BF16, name="gv", align_bytes=64)
+                else:
+                    g = gsp.tile([P, 2048], BF16, name="gs", align_bytes=64)
+                grouped[(i, c)] = g
+                if mk == "W1" and ORDER == "pair":
+                    dst = g[:].rearrange("p (k q j) -> p q j k", k=2, j=4)
+                    src = raw[i][:, :, c, :].rearrange("p j (q k) -> p q j k", k=2)
+                elif mk == "W1":
+                    dst = g[:].rearrange("p (t m u j) -> p m j u t", t=4, u=2, j=4)
+                    src = raw[i][:, :, c, :].rearrange("p j (m u t) -> p m j u t", u=2, t=4)
+                else:
+                    dst = g[:].rearrange("p (c i t) -> p c t i", i=4, t=4)
+                    src = raw[i][:, c, :, :].rearrange("p t (c i) -> p c t i", i=4)
+                if eng == "V":
+                    nc.vector.tensor_copy(out=dst, in_=src)
+                else:
+                    nc.scalar.copy(out=dst, in_=src)
+            elif kind == "q":
+                i, c = op[1], op[2]
+                mk, e = seq[i]
+                if i not in wc:
+                    wc[i] = codes.tile([P, 2048], U32, name="c_%d" % i, tag="c" + mk, align_bytes=64)
+                    ws[i] = codes.tile([P, 2048], U8, name="s_%d" % i, tag="s" + mk, align_bytes=64)
+                nc.vector.quantize_mx(out=wc[i][:, 512 * c:512 * c + 512].bitcast(FP8X4),
+                                      scales=ws[i][:, 512 * c:512 * c + 512], in_=grouped[(i, c)][:])
+            elif kind == "mm1":
+                e, g = op[1], op[2]
+                i = seq.index(("W1", e))
+                z = zp.tile([P, 4, P], F32, name="z", tag="z")
+                zt[(e, g)] = z
+                for t in range(4):
+                    lo = 512 * g + P * t
+                    nc.tensor.matmul_mx(out=z[:, t, :],
+                                        lhsT=wc[i][:, lo:lo + P].bitcast(FP8X4), lhsT_scale=ws[i][:, lo:lo + P],
+                                        rhs=xc[:, P * e:P * e + P].bitcast(FP8X4), rhs_scale=xs[:, P * e:P * e + P],
+                                        start=True, stop=True)
+            elif kind == "zout":
+                e, g = op[1], op[2]
+                if e not in hT:
+                    hT[e] = hp.tile([P, 4, 512], BF16, name="hT")
+                for tt in range(4):
+                    t = tt
+                    if ORDER == "pair":
+                        t = 2 * (tt % 2) + tt // 2
+                    nc.scalar.activation(out=hT[e][:, t, P * g:P * g + P], in_=zt[(e, g)][:, tt, :], func=ACT.Relu,
+                                         bias=b1T[:, t, 4 * e + g:4 * e + g + 1], scale=1.0)
+            elif kind == "hreg":
+                e = op[1]
+                hg[e] = hp.tile([P, 2048], BF16, name="hg", align_bytes=64)
+                nc.vector.tensor_copy(out=hg[e][:].rearrange("p (c i t) -> p c t i", i=4, t=4),
+                                      in_=hT[e][:].rearrange("p t (c i) -> p c t i", i=4))
+            elif kind == "hq":
+                e = op[1]
+                hc[e] = hp.tile([P, 512], U32, name="hc", align_bytes=64)
+                hs[e] = hp.tile([P, 512], U8, name="hs", align_bytes=64)
+                nc.vector.quantize_mx(out=hc[e][:].bitcast(FP8X4), scales=hs[e][:], in_=hg[e][:])
+            elif kind == "mm2":
+                e, c, first, last = op[1], op[2], op[3], op[4]
+                i = seq.index(("W2", e))
+                if first:
+                    yt[e] = yp.tile([P, D], F32, name="y")
+                nc.tensor.matmul_mx(out=yt[e][:],
+                                    lhsT=hc[e][:, P * c:P * c + P].bitcast(FP8X4), lhsT_scale=hs[e][:, P * c:P * c + P],
+                                    rhs=wc[i][:, 512 * c:512 * c + 512].bitcast(FP8X4),
+                                    rhs_scale=ws[i][:, 512 * c:512 * c + 512],
+                                    start=first, stop=last)
+            elif kind == "b2s":
+                e = op[1]
+                bs[e] = b2sp.tile([P, D], F32, name="bs")
+                nc.scalar.activation(out=bs[e][:], in_=pb[e][:].rearrange("p a b -> p (a b)"),
+                                     func=ACT.Copy, scale=s_col[:, 0:1])
+            elif kind == "b2p":
+                e = op[1]
+                pb[e] = zp.tile([P, 4, P], F32, name="pb", tag="z")
+                nc.tensor.matmul(out=pb[e][:].rearrange("p a b -> p (a b)"), lhsT=ones[:],
+                                 rhs=b2row[:, D * e:D * e + D], start=True, stop=True)
+            elif kind == "yout":
+                e = op[1]
+                ot[e] = outp.tile([P, D], F32, name="o_sb")
+                nc.vector.scalar_tensor_tensor(out=ot[e][:], in0=yt[e][:], scalar=s_col[:, 0:1],
+                                               in1=bs[e][:], op0=ALU.mult, op1=ALU.add)
+            elif kind == "st":
+                e = op[1]
+                nc.sync.dma_start(out=out[P * e:P * e + P, :], in_=ot[e][:])

@@ -175,7 +175,8 @@ def tile_moelayer_kernel(tc, x, W1, b1, W2, b2, temperature, out):
     seq, ops = make_plan()
     with ExitStack() as ctx:
         const = ctx.enter_context(tc.tile_pool(name="const", bufs=1))
-        rawp = ctx.enter_context(tc.tile_pool(name="raw", bufs=RAW_BUFS))
+        rawp = ctx.enter_context(tc.tile_pool(name="raw", bufs=2 * RAW_BUFS))
+        rawq = ctx.enter_context(tc.tile_pool(name="rawq", bufs=4))
         gvp = ctx.enter_context(tc.tile_pool(name="gvp", bufs=3))
         gsp = ctx.enter_context(tc.tile_pool(name="gsp", bufs=4))
         codes = ctx.enter_context(tc.tile_pool(name="codes", bufs=2))
@@ -237,21 +238,23 @@ def tile_moelayer_kernel(tc, x, W1, b1, W2, b2, temperature, out):
             elif kind == "ld":
                 i, a, b = op[1], op[2], op[3]
                 mk, e = seq[i]
-                if i not in raw:
-                    raw[i] = rawp.tile([P, 4, 4, 512], BF16, name="raw_%d" % i, tag="raw")
-                if mk == "W1":
-                    dst = raw[i][:].rearrange("p j g w -> p j (g w)")
-                    src = W1[e].rearrange("(p j) w -> p j w", j=4)
-                    nc.sync.dma_start(out=dst[:, :, 512 * a:512 * b], in_=src[:, :, 512 * a:512 * b])
+                n = b - a
+                if n == 1:
+                    piece = rawq.tile([P, 2048], BF16, name="raw_%d_%d" % (i, a), tag="rawq")
                 else:
-                    if ORDER == "pair":
-                        src = W2[e].rearrange("(a p k) d -> p a (k d)", p=P, k=2)
-                        dst = raw[i][:].rearrange("p g (u k) d -> p (g u) (k d)", u=2)
-                        nc.sync.dma_start(out=dst[:, 2 * a:2 * b, :], in_=src[:, 2 * a:2 * b, :])
-                    else:
-                        src = W2[e].rearrange("(g p t) d -> p g (t d)", p=P, t=4)
-                        dst = raw[i][:].rearrange("p g t d -> p g (t d)")
-                        nc.sync.dma_start(out=dst[:, a:b, :], in_=src[:, a:b, :])
+                    piece = rawp.tile([P, 4096], BF16, name="raw_%d_%d" % (i, a), tag="raw")
+                if mk == "W1":
+                    src = W1[e].rearrange("(p j) w -> p j w", j=4)
+                    rows = piece[:].rearrange("p (j w) -> p j w", j=4)
+                    nc.sync.dma_start(out=rows, in_=src[:, :, 512 * a:512 * b])
+                    for c in range(a, b):
+                        raw[(i, c)] = rows[:, :, 512 * (c - a):512 * (c - a) + 512]
+                else:
+                    src = W2[e].rearrange("(g p t) d -> p g (t d)", p=P, t=4)
+                    rows = piece[:].rearrange("p (g w) -> p g w", g=n)
+                    nc.sync.dma_start(out=rows, in_=src[:, a:b, :])
+                    for c in range(a, b):
+                        raw[(i, c)] = rows[:, c - a, :].rearrange("p (t d) -> p t d", t=4)
             elif kind == "ldx":
                 a, b = op[1], op[2]
                 nc.sync.dma_start(out=x_sb[:, a:b, :], in_=x_view[:, a:b, :])
@@ -293,15 +296,12 @@ def tile_moelayer_kernel(tc, x, W1, b1, W2, b2, temperature, out):
                 else:
                     g = gsp.tile([P, 2048], BF16, name="gs", align_bytes=64)
                 grouped[(i, c)] = g
-                if mk == "W1" and ORDER == "pair":
-                    dst = g[:].rearrange("p (k q j) -> p q j k", k=2, j=4)
-                    src = raw[i][:, :, c, :].rearrange("p j (q k) -> p q j k", k=2)
-                elif mk == "W1":
+                if mk == "W1":
                     dst = g[:].rearrange("p (t m u j) -> p m j u t", t=4, u=2, j=4)
-                    src = raw[i][:, :, c, :].rearrange("p j (m u t) -> p m j u t", u=2, t=4)
+                    src = raw[(i, c)].rearrange("p j (m u t) -> p m j u t", u=2, t=4)
                 else:
                     dst = g[:].rearrange("p (c i t) -> p c t i", i=4, t=4)
-                    src = raw[i][:, c, :, :].rearrange("p t (c i) -> p c t i", i=4)
+                    src = raw[(i, c)].rearrange("p t (c i) -> p c t i", i=4)
                 if eng == "V":
                     nc.vector.tensor_copy(out=dst, in_=src)
                 else:

@@ -14,26 +14,21 @@ ALU = mybir.AluOpType
 
 P = 128
 N_TOK, D, H = 1024, 512, 2048
+E = 8
 FLOPS = 2 * N_TOK * D * H * 2
 CLAMP_MAX = math.log(100.0)
-ORDER = "four"
-PINNED = True
 
-E = 8
-RAW_BUFS = 5
-
-
-V_EXTRA = (7,)
-S_EXTRA = ()
+AHEAD = 5
+V_EXTRA = ()
+PE_CHUNKS = ((3, 3), (5, 3), (7, 3), (9, 3), (11, 3), (15, 3))
 
 
-def make_plan(tail_swap=True, v_extra=V_EXTRA, s_extra=S_EXTRA):
+def make_plan():
     seq = []
     for e in range(E):
         seq.append(("W1", e))
         seq.append(("W2", e))
-    if tail_swap:
-        seq[13], seq[14] = seq[14], seq[13]
+    seq[13], seq[14] = seq[14], seq[13]
     where = dict((m, i) for i, m in enumerate(seq))
     n = len(seq)
     ops = []
@@ -41,9 +36,9 @@ def make_plan(tail_swap=True, v_extra=V_EXTRA, s_extra=S_EXTRA):
     z_wait = []
     z_done = [0] * E
     hreg_wait = []
-    hq_wait = []
     y_wait = []
     hq_done = []
+    hq_wait = []
     taken = [0, 0, 0, 0]
     hold = [False]
     passes = [[] for unused in range(E)]
@@ -60,14 +55,13 @@ def make_plan(tail_swap=True, v_extra=V_EXTRA, s_extra=S_EXTRA):
                         if len(passes[e]) == 4:
                             y_wait.append(e)
 
-    def q(i, c0, c1):
-        ops.append(("q", i, c0, c1))
+    def q(i, c):
+        ops.append(("q", i, c))
         kind, e = seq[i]
-        for c in range(c0, c1):
-            q_done[i].append(c)
-            if kind == "W1":
-                ops.append(("mm1", e, c))
-                z_wait.append((e, c))
+        q_done[i].append(c)
+        if kind == "W1":
+            ops.append(("mm1", e, c))
+            z_wait.append((e, c))
         try_mm2()
 
     def z_slot():
@@ -101,17 +95,26 @@ def make_plan(tail_swap=True, v_extra=V_EXTRA, s_extra=S_EXTRA):
             hq_done.append(e)
             try_mm2()
 
+    def cp(eng, i, c, lo=0, hi=512):
+        ops.append(("cp", "PE" if (i, c) in PE_CHUNKS else eng, i, c, lo, hi))
+
+    def ld(i):
+        if i == 0:
+            cuts = (0, 256, 512, 1024, 1536, 2048)
+        elif seq[i][0] == "W1":
+            cuts = (0, 1024, 2048)
+        else:
+            cuts = (0, 512, 1024, 1536, 2048)
+        for lo, hi in zip(cuts, cuts[1:]):
+            if (i, lo) == (0, 1536):
+                ops.append(("ldx", 0, 2))
+            ops.append(("ld", i, lo, hi))
+
     ops.append(("ldsmall",))
-    ops.append(("ld", 0, 0, 1))
-    ops.append(("ld", 0, 1, 2))
-    ops.append(("ldx", 0, 2))
-    ops.append(("ld", 0, 2, 3))
-    ops.append(("ld", 0, 3, 4))
-    for i in range(1, RAW_BUFS):
-        ops.append(("ld", i, 0, 2))
-        if i == 2:
+    for i in range(AHEAD):
+        if i == 3:
             ops.append(("ldx", 2, 4))
-        ops.append(("ld", i, 2, 4))
+        ld(i)
     b2 = [0, 0]
     for i in range(n + 1):
         last = i >= n - 1
@@ -126,42 +129,59 @@ def make_plan(tail_swap=True, v_extra=V_EXTRA, s_extra=S_EXTRA):
             b2[1] += 1
         if i in (2, 6, 10):
             ops.append(("xtp", i // 2 + 1, i // 2 + 3))
-        if i < n:
-            ops.append(("cp", "S", i, 1, 2))
-            ops.append(("cp", "V", i, 0, 1))
         if i == 0:
+            cp("V", 0, 0, 0, 256)
+            cp("S", 0, 0, 256, 512)
+            cp("V", 0, 1)
+            cp("S", 0, 2)
+            ops.append(("q", 0, 0))
+            q_done[0].append(0)
+            ops.append(("q", 0, 1))
+            q_done[0].append(1)
             ops.append(("consts",))
             ops.append(("exp",))
             ops.append(("xtp", 0, 2))
+            cp("V", 0, 3)
             ops.append(("xcp", 0, 2))
+        elif i < n:
+            cp("S", i, 1)
+            cp("V", i, 0)
+            cp("V", i, 2)
+            cp("V" if i in V_EXTRA else "S", i, 3)
         if i < n:
-            ops.append(("cp", "S" if i in s_extra else "V", i, 2, 3))
-            ops.append(("cp", "V" if i in v_extra else "S", i, 3, 4))
             if i in (1, 5):
                 ops.append(("ldx", (i + 7) // 2, (i + 7) // 2 + 2))
-            if i + RAW_BUFS < n:
-                ops.append(("ld", i + RAW_BUFS, 0, 2))
-                ops.append(("ld", i + RAW_BUFS, 2, 4))
+            if i + AHEAD < n:
+                ld(i + AHEAD)
         hreg_slot(h_ready)
         if i == 0:
             ops.append(("b1T",))
             ops.append(("xq", 0, 2))
+            for c in (0, 1):
+                ops.append(("mm1", 0, c))
+                z_wait.append((0, c))
         if i in (3, 7, 11):
             ops.append(("xcp", (i + 1) // 2, (i + 1) // 2 + 2))
-        if i > 0:
-            q(i - 1, 3, 4)
+        if i > 1:
+            q(i - 1, 3)
         z_slot()
         hold[0] = False
         try_mm2()
         hold[0] = not last
         if i in (4, 8, 12):
             ops.append(("xq", i // 2, i // 2 + 2))
-        if i < n:
-            q(i, 0, 1)
-            q(i, 2, 3)
+        if i == 0:
+            q(0, 2)
+            q(0, 3)
+        elif i < n:
+            q(i, 0)
+            q(i, 2)
         hq_slot()
-        if i < n:
-            q(i, 1, 2)
+        if 0 < i < n:
+            q(i, 1)
+        for (m, c) in PE_CHUNKS:
+            if m == i + 1:
+                ops.append(("pe", m, c))
         y_slot(y_ready)
     hold[0] = False
     hreg_slot(len(hreg_wait))
@@ -175,18 +195,16 @@ def tile_moelayer_kernel(tc, x, W1, b1, W2, b2, temperature, out):
     seq, ops = make_plan()
     with ExitStack() as ctx:
         const = ctx.enter_context(tc.tile_pool(name="const", bufs=1))
-        rawp = ctx.enter_context(tc.tile_pool(name="raw", bufs=2 * RAW_BUFS))
-        rawq = ctx.enter_context(tc.tile_pool(name="rawq", bufs=4))
-        gvp = ctx.enter_context(tc.tile_pool(name="gvp", bufs=3))
-        gsp = ctx.enter_context(tc.tile_pool(name="gsp", bufs=4))
+        rawp = ctx.enter_context(tc.tile_pool(name="raw", bufs=5))
+        rawq = ctx.enter_context(tc.tile_pool(name="rawq", bufs=12))
+        gp = ctx.enter_context(tc.tile_pool(name="gp", bufs=7))
         codes = ctx.enter_context(tc.tile_pool(name="codes", bufs=2))
         hp = ctx.enter_context(tc.tile_pool(name="hp", bufs=2))
         outp = ctx.enter_context(tc.tile_pool(name="outp", bufs=3))
         b2sp = ctx.enter_context(tc.tile_pool(name="b2sp", bufs=2))
         zp = ctx.enter_context(tc.psum_pool(name="zp", bufs=6))
         yp = ctx.enter_context(tc.psum_pool(name="yp", bufs=2))
-        if PINNED:
-            ctx.enter_context(tc.manual_schedule())
+        ctx.enter_context(tc.manual_schedule())
 
         raw = {}
         grouped = {}
@@ -202,6 +220,7 @@ def tile_moelayer_kernel(tc, x, W1, b1, W2, b2, temperature, out):
         held = {}
         pb = {}
         bs = {}
+        pt = {}
 
         x_sb = const.tile([P, E, D], BF16, name="x_sb")
         xg = const.tile([P, E * P * 4], BF16, name="xg", align_bytes=64)
@@ -217,8 +236,8 @@ def tile_moelayer_kernel(tc, x, W1, b1, W2, b2, temperature, out):
         b1_g = const.tile([P, 4, P], BF16, name="b1_g")
         b1T = const.tile([P, 4, 32], F32, name="b1T")
         warm = const.tile([P, 2], F32, name="warm")
-        b2row = const.tile([P, E * D], BF16, name="b2row")
-        ones = const.tile([P, P], BF16, name="ones")
+        b2_raw = const.tile([P, P], BF16, name="b2_raw")
+        b2T = const.tile([P, 32], F32, name="b2T")
         ident_f = const.tile([P, P], F32, name="ident_f")
         ident_b = const.tile([P, P], BF16, name="ident_b")
 
@@ -227,50 +246,47 @@ def tile_moelayer_kernel(tc, x, W1, b1, W2, b2, temperature, out):
             if kind == "ldsmall":
                 nc.vector.memset(warm[:], 0.0)
                 nc.vector.memset(b1_raw[:], 0.0)
+                nc.vector.memset(b2_raw[:], 0.0)
                 nc.scalar.dma_start(out=t_sb[:], in_=temperature.partition_broadcast(P))
                 nc.scalar.dma_start(out=b1_raw[0:32, :], in_=b1.rearrange("e (g f) -> (e g) f", g=4))
+                nc.scalar.dma_start(out=b2_raw[0:32, :], in_=b2.rearrange("e (q f) -> (e q) f", q=4))
                 nc.scalar.activation(out=warm[:, 1:2], in_=warm[:, 0:1], func=ACT.Exp)
                 make_identity(nc, ident_f[:])
                 make_identity(nc, ident_b[:])
-                nc.gpsimd.memset(b2row[:].bitcast(F32), 0.0)
-                nc.gpsimd.memset(ones[:], 1.0)
-                nc.gpsimd.dma_start(out=b2row[0:1, :], in_=b2.rearrange("(o e) d -> o (e d)", o=1))
             elif kind == "ld":
                 i, a, b = op[1], op[2], op[3]
                 mk, e = seq[i]
                 n = b - a
-                if n == 1:
-                    piece = rawq.tile([P, 2048], BF16, name="raw_%d_%d" % (i, a), tag="rawq")
+                if n < 1024:
+                    piece = rawq.tile([P, 4 * n], BF16, name="raw_%d_%d" % (i, a), tag="rawq")
                 else:
-                    piece = rawp.tile([P, 4096], BF16, name="raw_%d_%d" % (i, a), tag="raw")
+                    piece = rawp.tile([P, 4 * n], BF16, name="raw_%d_%d" % (i, a), tag="raw")
                 if mk == "W1":
                     src = W1[e].rearrange("(p j) w -> p j w", j=4)
                     rows = piece[:].rearrange("p (j w) -> p j w", j=4)
-                    nc.sync.dma_start(out=rows, in_=src[:, :, 512 * a:512 * b])
-                    for c in range(a, b):
-                        raw[(i, c)] = rows[:, :, 512 * (c - a):512 * (c - a) + 512]
+                    nc.sync.dma_start(out=rows, in_=src[:, :, a:b])
+                    for lo in range(a, b, 256):
+                        raw[(i, lo)] = (rows, lo - a)
                 else:
                     src = W2[e].rearrange("(g p t) d -> p g (t d)", p=P, t=4)
-                    rows = piece[:].rearrange("p (g w) -> p g w", g=n)
-                    nc.sync.dma_start(out=rows, in_=src[:, a:b, :])
-                    for c in range(a, b):
-                        raw[(i, c)] = rows[:, c - a, :].rearrange("p (t d) -> p t d", t=4)
+                    rows = piece[:].rearrange("p (g w) -> p g w", g=n // 512)
+                    nc.sync.dma_start(out=rows, in_=src[:, a // 512:b // 512, :])
+                    for lo in range(a, b, 256):
+                        raw[(i, lo)] = (rows[:, (lo - a) // 512, :].rearrange("p (t d) -> p t d", t=4), lo % 512)
             elif kind == "ldx":
                 a, b = op[1], op[2]
                 nc.sync.dma_start(out=x_sb[:, a:b, :], in_=x_view[:, a:b, :])
             elif kind == "consts":
                 nc.vector.tensor_scalar_min(out=t_min[:], in0=t_sb[:], scalar1=CLAMP_MAX)
-                if ORDER == "pair":
-                    nc.vector.tensor_copy(out=b1_g[:].rearrange("p (u k) m -> p u k m", u=2),
-                                          in_=b1_raw[:].rearrange("p (u m k) -> p u k m", u=2, k=2))
-                else:
-                    nc.vector.tensor_copy(out=b1_g[:], in_=b1_raw[:].rearrange("p (m t) -> p t m", t=4))
-                b1_ps = zp.tile([P, 4, P], BF16, name="b1_ps", tag="z")
+                nc.vector.tensor_copy(out=b1_g[:], in_=b1_raw[:].rearrange("p (m t) -> p t m", t=4))
+                b1_ps = zp.tile([P, 5, P], BF16, name="b1_ps", tag="z")
                 for t in range(4):
                     nc.tensor.transpose(b1_ps[:, t, :], b1_g[:, t, :], ident_b[:])
+                nc.tensor.transpose(b1_ps[:, 4, :], b2_raw[:], ident_b[:])
                 held["b1_ps"] = b1_ps
             elif kind == "b1T":
-                nc.vector.tensor_copy(out=b1T[:], in_=held["b1_ps"][:, :, 0:32])
+                nc.vector.tensor_copy(out=b1T[:], in_=held["b1_ps"][:, 0:4, 0:32])
+                nc.vector.tensor_scalar_mul(out=b2T[:], in0=held["b1_ps"][:, 4, 0:32], scalar1=s_col[:, 0:1])
             elif kind == "exp":
                 nc.scalar.activation(out=s_col[:], in_=t_min[:], func=ACT.Exp)
             elif kind == "xtp":
@@ -288,24 +304,38 @@ def tile_moelayer_kernel(tc, x, W1, b1, W2, b2, temperature, out):
                 a, b = op[1], op[2]
                 nc.vector.quantize_mx(out=xc[:, P * a:P * b].bitcast(FP8X4), scales=xs[:, P * a:P * b],
                                       in_=xg[:, 4 * P * a:4 * P * b])
+            elif kind == "pe":
+                i, c = op[1], op[2]
+                rows, first = raw[(i, 512 * c)]
+                for half in range(2):
+                    pt[(i, c, half)] = zp.tile([P, 1024], BF16, name="pt", tag="z")
+                    for part in range(2):
+                        lo = first + 256 * half + 128 * part
+                        nc.tensor.matmul(out=pt[(i, c, half)][:, 512 * part:512 * part + 512], lhsT=ident_b[:],
+                                         rhs=rows[:, :, lo:lo + P].rearrange("p t d -> p d t"),
+                                         start=True, stop=True)
             elif kind == "cp":
-                eng, i, c = op[1], op[2], op[3]
+                eng, i, c, lo, hi = op[1:]
                 mk, e = seq[i]
-                if eng == "V":
-                    g = gvp.tile([P, 2048], BF16, name="gv", align_bytes=64)
+                if (i, c) not in grouped:
+                    grouped[(i, c)] = gp.tile([P, 2048], BF16, name="g", align_bytes=64)
+                g = grouped[(i, c)]
+                if eng == "PE":
+                    for half in range(2):
+                        nc.scalar.copy(out=g[:, 1024 * half:1024 * half + 1024], in_=pt[(i, c, half)][:])
                 else:
-                    g = gsp.tile([P, 2048], BF16, name="gs", align_bytes=64)
-                grouped[(i, c)] = g
-                if mk == "W1":
-                    dst = g[:].rearrange("p (t m u j) -> p m j u t", t=4, u=2, j=4)
-                    src = raw[(i, c)].rearrange("p j (m u t) -> p m j u t", u=2, t=4)
-                else:
-                    dst = g[:].rearrange("p (c i t) -> p c t i", i=4, t=4)
-                    src = raw[(i, c)].rearrange("p t (c i) -> p c t i", i=4)
-                if eng == "V":
-                    nc.vector.tensor_copy(out=dst, in_=src)
-                else:
-                    nc.scalar.copy(out=dst, in_=src)
+                    rows, first = raw[(i, 512 * c + lo)]
+                    part = rows[:, :, first:first + hi - lo]
+                    if mk == "W1":
+                        dst = g[:].rearrange("p (t m u j) -> p m j u t", t=4, u=2, j=4)[:, lo // 8:hi // 8]
+                        src = part.rearrange("p j (m u t) -> p m j u t", u=2, t=4)
+                    else:
+                        dst = g[:].rearrange("p (c i t) -> p c t i", i=4, t=4)[:, lo // 4:hi // 4]
+                        src = part.rearrange("p t (c i) -> p c t i", i=4)
+                    if eng == "V":
+                        nc.vector.tensor_copy(out=dst, in_=src)
+                    else:
+                        nc.scalar.copy(out=dst, in_=src)
             elif kind == "q":
                 i, c = op[1], op[2]
                 mk, e = seq[i]
@@ -329,11 +359,8 @@ def tile_moelayer_kernel(tc, x, W1, b1, W2, b2, temperature, out):
                 e, g = op[1], op[2]
                 if e not in hT:
                     hT[e] = hp.tile([P, 4, 512], BF16, name="hT")
-                for tt in range(4):
-                    t = tt
-                    if ORDER == "pair":
-                        t = 2 * (tt % 2) + tt // 2
-                    nc.scalar.activation(out=hT[e][:, t, P * g:P * g + P], in_=zt[(e, g)][:, tt, :], func=ACT.Relu,
+                for t in range(4):
+                    nc.scalar.activation(out=hT[e][:, t, P * g:P * g + P], in_=zt[(e, g)][:, t, :], func=ACT.Relu,
                                          bias=b1T[:, t, 4 * e + g:4 * e + g + 1], scale=1.0)
             elif kind == "hreg":
                 e = op[1]
@@ -358,13 +385,12 @@ def tile_moelayer_kernel(tc, x, W1, b1, W2, b2, temperature, out):
             elif kind == "b2s":
                 e = op[1]
                 bs[e] = b2sp.tile([P, D], F32, name="bs")
-                nc.scalar.activation(out=bs[e][:], in_=pb[e][:].rearrange("p a b -> p (a b)"),
-                                     func=ACT.Copy, scale=s_col[:, 0:1])
+                nc.scalar.copy(out=bs[e][:], in_=pb[e][:].rearrange("p a b -> p (a b)"))
             elif kind == "b2p":
                 e = op[1]
                 pb[e] = zp.tile([P, 4, P], F32, name="pb", tag="z")
-                nc.tensor.matmul(out=pb[e][:].rearrange("p a b -> p (a b)"), lhsT=ones[:],
-                                 rhs=b2row[:, D * e:D * e + D], start=True, stop=True)
+                for q4 in range(4):
+                    nc.tensor.transpose(pb[e][:, q4, :], b2T[:, 4 * e + q4:4 * e + q4 + 1].to_broadcast([P, P]), ident_f[:])
             elif kind == "yout":
                 e = op[1]
                 ot[e] = outp.tile([P, D], F32, name="o_sb")

@@ -19,16 +19,16 @@ FLOPS = 2 * N_TOK * D * H * 2
 CLAMP_MAX = math.log(100.0)
 
 AHEAD = 5
-V_EXTRA = ()
-PE_CHUNKS = ((3, 3), (5, 3), (7, 3), (9, 3), (11, 3), (15, 3))
+V_MORE = (1, 2)
+PE_HALF = (2, 3, 4, 5, 6, 7, 8, 10, 12, 13, 14, 15)
 
 
 def make_plan():
-    seq = []
-    for e in range(E):
+    seq = [("W1", 0)]
+    for e in range(1, E):
         seq.append(("W1", e))
-        seq.append(("W2", e))
-    seq[13], seq[14] = seq[14], seq[13]
+        seq.append(("W2", e - 1))
+    seq.append(("W2", E - 1))
     where = dict((m, i) for i, m in enumerate(seq))
     n = len(seq)
     ops = []
@@ -55,13 +55,14 @@ def make_plan():
                         if len(passes[e]) == 4:
                             y_wait.append(e)
 
-    def q(i, c):
-        ops.append(("q", i, c))
+    def q(i, c0, c1, mm=True):
+        ops.append(("q", i, c0, c1))
         kind, e = seq[i]
-        q_done[i].append(c)
-        if kind == "W1":
-            ops.append(("mm1", e, c))
-            z_wait.append((e, c))
+        for c in range(c0, c1):
+            q_done[i].append(c)
+            if kind == "W1" and mm:
+                ops.append(("mm1", e, c))
+                z_wait.append((e, c))
         try_mm2()
 
     def z_slot():
@@ -80,8 +81,8 @@ def make_plan():
             ops.append(("yout", e))
             ops.append(("st", e))
 
-    def hreg_slot(limit):
-        while taken[2] < limit:
+    def hreg_slot(i):
+        while taken[2] < len(hreg_wait) and where[("W2", hreg_wait[taken[2]])] <= i:
             e = hreg_wait[taken[2]]
             taken[2] += 1
             ops.append(("hreg", e))
@@ -96,7 +97,11 @@ def make_plan():
             try_mm2()
 
     def cp(eng, i, c, lo=0, hi=512):
-        ops.append(("cp", "PE" if (i, c) in PE_CHUNKS else eng, i, c, lo, hi))
+        if c == 3 and i in PE_HALF:
+            ops.append(("cp", eng, i, 3, 0, 256))
+            ops.append(("cp", "PE", i, 3, 256, 512))
+        else:
+            ops.append(("cp", eng, i, c, lo, hi))
 
     def ld(i):
         if i == 0:
@@ -112,13 +117,12 @@ def make_plan():
 
     ops.append(("ldsmall",))
     for i in range(AHEAD):
-        if i == 3:
+        if i == 2:
             ops.append(("ldx", 2, 4))
         ld(i)
     b2 = [0, 0]
     for i in range(n + 1):
         last = i >= n - 1
-        h_ready = len(hreg_wait)
         y_ready = len(y_wait)
         hold[0] = not last
         if i >= 3 and b2[0] < E and (i % 2 == 1 or i == n - 2):
@@ -127,64 +131,65 @@ def make_plan():
         if i >= 2 and b2[1] < E and (i % 2 == 0 or i == n - 3):
             ops.append(("b2p", b2[1]))
             b2[1] += 1
-        if i in (2, 6, 10):
-            ops.append(("xtp", i // 2 + 1, i // 2 + 3))
+        if i in (1, 5, 9):
+            ops.append(("xtp", i // 2 + 2, i // 2 + 4))
         if i == 0:
             cp("V", 0, 0, 0, 256)
             cp("S", 0, 0, 256, 512)
             cp("V", 0, 1)
             cp("S", 0, 2)
-            ops.append(("q", 0, 0))
-            q_done[0].append(0)
-            ops.append(("q", 0, 1))
-            q_done[0].append(1)
             ops.append(("consts",))
             ops.append(("exp",))
             ops.append(("xtp", 0, 2))
+            q(0, 0, 2, False)
             cp("V", 0, 3)
             ops.append(("xcp", 0, 2))
         elif i < n:
-            cp("S", i, 1)
+            if i in V_MORE:
+                cp("S", i, 2, 256, 512)
+            else:
+                cp("S", i, 2)
             cp("V", i, 0)
-            cp("V", i, 2)
-            cp("V" if i in V_EXTRA else "S", i, 3)
+            cp("V", i, 1)
+            if i in V_MORE:
+                cp("V", i, 2, 0, 256)
+            cp("S", i, 3)
         if i < n:
             if i in (1, 5):
                 ops.append(("ldx", (i + 7) // 2, (i + 7) // 2 + 2))
             if i + AHEAD < n:
                 ld(i + AHEAD)
-        hreg_slot(h_ready)
         if i == 0:
             ops.append(("b1T",))
             ops.append(("xq", 0, 2))
             for c in (0, 1):
                 ops.append(("mm1", 0, c))
                 z_wait.append((0, c))
-        if i in (3, 7, 11):
-            ops.append(("xcp", (i + 1) // 2, (i + 1) // 2 + 2))
+        if i in (2, 6, 10):
+            ops.append(("xcp", i // 2 + 1, i // 2 + 3))
         if i > 1:
-            q(i - 1, 3)
+            if i == n:
+                q(i - 1, 2, 3)
+                q(i - 1, 3, 4)
+            else:
+                q(i - 1, 2, 4)
+        hreg_slot(i)
         z_slot()
         hold[0] = False
         try_mm2()
         hold[0] = not last
-        if i in (4, 8, 12):
-            ops.append(("xq", i // 2, i // 2 + 2))
+        if i in (3, 7, 11):
+            ops.append(("xq", (i + 1) // 2, (i + 1) // 2 + 2))
         if i == 0:
-            q(0, 2)
-            q(0, 3)
+            q(0, 2, 4)
         elif i < n:
-            q(i, 0)
-            q(i, 2)
+            q(i, 0, 2)
         hq_slot()
-        if 0 < i < n:
-            q(i, 1)
-        for (m, c) in PE_CHUNKS:
-            if m == i + 1:
-                ops.append(("pe", m, c))
+        if i + 1 in PE_HALF:
+            ops.append(("pe", i + 1))
         y_slot(y_ready)
     hold[0] = False
-    hreg_slot(len(hreg_wait))
+    hreg_slot(n)
     hq_slot()
     y_slot(len(y_wait))
     return seq, ops
@@ -197,7 +202,7 @@ def tile_moelayer_kernel(tc, x, W1, b1, W2, b2, temperature, out):
         const = ctx.enter_context(tc.tile_pool(name="const", bufs=1))
         rawp = ctx.enter_context(tc.tile_pool(name="raw", bufs=5))
         rawq = ctx.enter_context(tc.tile_pool(name="rawq", bufs=12))
-        gp = ctx.enter_context(tc.tile_pool(name="gp", bufs=7))
+        gp = ctx.enter_context(tc.tile_pool(name="gp", bufs=4))
         codes = ctx.enter_context(tc.tile_pool(name="codes", bufs=2))
         hp = ctx.enter_context(tc.tile_pool(name="hp", bufs=2))
         outp = ctx.enter_context(tc.tile_pool(name="outp", bufs=3))
@@ -305,45 +310,52 @@ def tile_moelayer_kernel(tc, x, W1, b1, W2, b2, temperature, out):
                 nc.vector.quantize_mx(out=xc[:, P * a:P * b].bitcast(FP8X4), scales=xs[:, P * a:P * b],
                                       in_=xg[:, 4 * P * a:4 * P * b])
             elif kind == "pe":
-                i, c = op[1], op[2]
-                rows, first = raw[(i, 512 * c)]
-                for half in range(2):
-                    pt[(i, c, half)] = zp.tile([P, 1024], BF16, name="pt", tag="z")
-                    for part in range(2):
-                        lo = first + 256 * half + 128 * part
-                        nc.tensor.matmul(out=pt[(i, c, half)][:, 512 * part:512 * part + 512], lhsT=ident_b[:],
-                                         rhs=rows[:, :, lo:lo + P].rearrange("p t d -> p d t"),
-                                         start=True, stop=True)
+                i = op[1]
+                mk, e = seq[i]
+                rows, first = raw[(i, 1792)]
+                pt[i] = zp.tile([P, 1024], BF16, name="pt", tag="z")
+                for part in range(2):
+                    if mk == "W1":
+                        src = rows[:, :, first:first + 256].rearrange("p j (m t) -> p t m j", t=4)[:, 2 * part:2 * part + 2]
+                    else:
+                        src = rows[:, :, first + P * part:first + P * part + P].rearrange("p t d -> p d t")
+                    nc.tensor.matmul(out=pt[i][:, 512 * part:512 * part + 512], lhsT=ident_b[:], rhs=src,
+                                     start=True, stop=True)
             elif kind == "cp":
                 eng, i, c, lo, hi = op[1:]
                 mk, e = seq[i]
-                if (i, c) not in grouped:
-                    grouped[(i, c)] = gp.tile([P, 2048], BF16, name="g", align_bytes=64)
-                g = grouped[(i, c)]
+                if (i, c // 2) not in grouped:
+                    grouped[(i, c // 2)] = gp.tile([P, 4096], BF16, name="g", align_bytes=64)
+                g = grouped[(i, c // 2)][:, 2048 * (c % 2):2048 * (c % 2) + 2048]
                 if eng == "PE":
-                    for half in range(2):
-                        nc.scalar.copy(out=g[:, 1024 * half:1024 * half + 1024], in_=pt[(i, c, half)][:])
+                    if mk == "W1":
+                        nc.scalar.copy(out=g.rearrange("p (t w) -> p t w", t=4)[:, :, 256:512],
+                                       in_=pt[i][:].rearrange("p (t w) -> p t w", t=4))
+                    else:
+                        nc.scalar.copy(out=g[:, 1024:2048], in_=pt[i][:])
                 else:
                     rows, first = raw[(i, 512 * c + lo)]
                     part = rows[:, :, first:first + hi - lo]
                     if mk == "W1":
-                        dst = g[:].rearrange("p (t m u j) -> p m j u t", t=4, u=2, j=4)[:, lo // 8:hi // 8]
+                        dst = g.rearrange("p (t m u j) -> p m j u t", t=4, u=2, j=4)[:, lo // 8:hi // 8]
                         src = part.rearrange("p j (m u t) -> p m j u t", u=2, t=4)
                     else:
-                        dst = g[:].rearrange("p (c i t) -> p c t i", i=4, t=4)[:, lo // 4:hi // 4]
+                        dst = g.rearrange("p (c i t) -> p c t i", i=4, t=4)[:, lo // 4:hi // 4]
                         src = part.rearrange("p t (c i) -> p c t i", i=4)
                     if eng == "V":
                         nc.vector.tensor_copy(out=dst, in_=src)
                     else:
                         nc.scalar.copy(out=dst, in_=src)
             elif kind == "q":
-                i, c = op[1], op[2]
+                i, c0, c1 = op[1:]
                 mk, e = seq[i]
                 if i not in wc:
                     wc[i] = codes.tile([P, 2048], U32, name="c_%d" % i, tag="c" + mk, align_bytes=64)
                     ws[i] = codes.tile([P, 2048], U8, name="s_%d" % i, tag="s" + mk, align_bytes=64)
-                nc.vector.quantize_mx(out=wc[i][:, 512 * c:512 * c + 512].bitcast(FP8X4),
-                                      scales=ws[i][:, 512 * c:512 * c + 512], in_=grouped[(i, c)][:])
+                first = 2048 * (c0 % 2)
+                nc.vector.quantize_mx(out=wc[i][:, 512 * c0:512 * c1].bitcast(FP8X4),
+                                      scales=ws[i][:, 512 * c0:512 * c1],
+                                      in_=grouped[(i, c0 // 2)][:, first:first + 2048 * (c1 - c0)])
             elif kind == "mm1":
                 e, g = op[1], op[2]
                 i = seq.index(("W1", e))

@@ -336,6 +336,12 @@ def tile_moelayer_kernel(tc, x, W1, b1, W2, b2, temperature, out):
                 else:
                     rows, first = raw[(i, 512 * c + lo)]
                     part = rows[:, :, first:first + hi - lo]
+                    if mk == "W1" and eng == "V":
+                        dst = g.rearrange("p (h l m u j) -> p h m j u l", h=2, l=2, u=2, j=4)[:, :, lo // 8:hi // 8]
+                        src = part.rearrange("p j (m u h l) -> p h m j u l", u=2, h=2, l=2)
+                        for h in range(2):
+                            nc.vector.tensor_copy(out=dst[:, h], in_=src[:, h])
+                        continue
                     if mk == "W1":
                         dst = g.rearrange("p (t m u j) -> p m j u t", t=4, u=2, j=4)[:, lo // 8:hi // 8]
                         src = part.rearrange("p j (m u t) -> p m j u t", u=2, t=4)

@@ -346,8 +346,9 @@ def tile_moelayer_kernel(tc, x, W1, b1, W2, b2, temperature, out):
                         dst = g.rearrange("p (t m u j) -> p m j u t", t=4, u=2, j=4)[:, lo // 8:hi // 8]
                         src = part.rearrange("p j (m u t) -> p m j u t", u=2, t=4)
                     else:
-                        dst = g.rearrange("p (c i t) -> p c t i", i=4, t=4)[:, lo // 4:hi // 4]
-                        src = part.rearrange("p t (c i) -> p c t i", i=4)
+                        run = 2 if eng == "V" else 4
+                        dst = g.rearrange("p (c i t) -> p c t i", i=run, t=4)[:, lo // run:hi // run]
+                        src = part.rearrange("p t (c i) -> p c t i", i=run)
                     if eng == "V":
                         nc.vector.tensor_copy(out=dst, in_=src)
                     else:
@@ -383,8 +384,8 @@ def tile_moelayer_kernel(tc, x, W1, b1, W2, b2, temperature, out):
             elif kind == "hreg":
                 e = op[1]
                 hg[e] = hp.tile([P, 2048], BF16, name="hg", align_bytes=64)
-                nc.vector.tensor_copy(out=hg[e][:].rearrange("p (c i t) -> p c t i", i=4, t=4),
-                                      in_=hT[e][:].rearrange("p t (c i) -> p c t i", i=4))
+                nc.vector.tensor_copy(out=hg[e][:].rearrange("p (c i t) -> p c t i", i=2, t=4),
+                                      in_=hT[e][:].rearrange("p t (c i) -> p c t i", i=2))
             elif kind == "hq":
                 e = op[1]
                 hc[e] = hp.tile([P, 512], U32, name="hc", align_bytes=64)

@@ -315,12 +315,14 @@ def tile_moelayer_kernel(tc, x, W1, b1, W2, b2, temperature, out):
                 rows, first = raw[(i, 1792)]
                 pt[i] = zp.tile([P, 1024], BF16, name="pt", tag="z")
                 for part in range(2):
+                    lo = first + P * part
                     if mk == "W1":
-                        src = rows[:, :, first:first + 256].rearrange("p j (m t) -> p t m j", t=4)[:, 2 * part:2 * part + 2]
+                        src = rows[:, :, lo:lo + P].rearrange("p j (m t) -> p j m t", t=4)
+                        dst = pt[i][:].rearrange("p (t m j) -> p j m t", t=4, j=4)[:, :, 32 * part:32 * part + 32]
                     else:
-                        src = rows[:, :, first + P * part:first + P * part + P].rearrange("p t d -> p d t")
-                    nc.tensor.matmul(out=pt[i][:, 512 * part:512 * part + 512], lhsT=ident_b[:], rhs=src,
-                                     start=True, stop=True)
+                        src = rows[:, :, lo:lo + P]
+                        dst = pt[i][:].rearrange("p (d t) -> p t d", t=4)[:, :, P * part:P * part + P]
+                    nc.tensor.matmul(out=dst, lhsT=ident_b[:], rhs=src, start=True, stop=True)
             elif kind == "cp":
                 eng, i, c, lo, hi = op[1:]
                 mk, e = seq[i]

import math
from contextlib import ExitStack

import concourse.mybir as mybir
from concourse.masks import make_identity

FP8X4 = mybir.dt.float8_e4m3fn_x4
BF16 = mybir.dt.bfloat16
F32 = mybir.dt.float32
U32 = mybir.dt.uint32
U8 = mybir.dt.uint8
ACT = mybir.ActivationFunctionType
ALU = mybir.AluOpType

P = 128
N_TOK, D, H = 1024, 512, 2048
E = 8
FLOPS = 2 * N_TOK * D * H * 2
CLAMP_MAX = math.log(100.0)

AHEAD = 5
V_MORE = (1, 2)
PE_HALF = (2, 3, 4, 5, 6, 7, 8, 10, 12, 13, 14, 15)


def make_plan():
    seq = [("W1", 0)]
    for e in range(1, E):
        seq.append(("W1", e))
        seq.append(("W2", e - 1))
    seq.append(("W2", E - 1))
    where = dict((m, i) for i, m in enumerate(seq))
    n = len(seq)
    ops = []
    q_done = [[] for unused in range(n)]
    z_wait = []
    z_done = [0] * E
    hreg_wait = []
    y_wait = []
    hq_done = []
    hq_wait = []
    taken = [0, 0, 0, 0]
    hold = [False]
    passes = [[] for unused in range(E)]

    def try_mm2():
        if hold[0]:
            return
        for e in range(E):
            if e in hq_done:
                for c in q_done[where[("W2", e)]]:
                    if c not in passes[e]:
                        passes[e].append(c)
                        ops.append(("mm2", e, c, len(passes[e]) == 1, len(passes[e]) == 4))
                        if len(passes[e]) == 4:
                            y_wait.append(e)

    def q(i, c0, c1, mm=True):
        ops.append(("q", i, c0, c1))
        kind, e = seq[i]
        for c in range(c0, c1):
            q_done[i].append(c)
            if kind == "W1" and mm:
                ops.append(("mm1", e, c))
                z_wait.append((e, c))
        try_mm2()

    def z_slot():
        while taken[0] < len(z_wait):
            e, g = z_wait[taken[0]]
            taken[0] += 1
            ops.append(("zout", e, g))
            z_done[e] += 1
            if z_done[e] == 4:
                hreg_wait.append(e)

    def y_slot(limit):
        while taken[1] < limit:
            e = y_wait[taken[1]]
            taken[1] += 1
            ops.append(("yout", e))
            ops.append(("st", e))

    def hreg_slot(i):
        while taken[2] < len(hreg_wait) and where[("W2", hreg_wait[taken[2]])] <= i:
            e = hreg_wait[taken[2]]
            taken[2] += 1
            ops.append(("hreg", e))
            hq_wait.append(e)

    def hq_slot():
        while taken[3] < len(hq_wait):
            e = hq_wait[taken[3]]
            taken[3] += 1
            ops.append(("hq", e))
            hq_done.append(e)
            try_mm2()

    def cp(eng, i, c, lo=0, hi=512):
        if c == 3 and i in PE_HALF:
            ops.append(("cp", eng, i, 3, 0, 256))
            ops.append(("cp", "PE", i, 3, 256, 512))
        else:
            ops.append(("cp", eng, i, c, lo, hi))

    def ld(i):
        if i == 0:
            cuts = (0, 256, 512, 1024, 1536, 2048)
        elif seq[i][0] == "W1":
            cuts = (0, 1024, 2048)
        else:
            cuts = (0, 512, 1024, 1536, 2048)
        for lo, hi in zip(cuts, cuts[1:]):
            if (i, lo) == (0, 1536):
                ops.append(("ldx", 0, 2))
            ops.append(("ld", i, lo, hi))

    ops.append(("ldsmall",))
    for i in range(AHEAD):
        if i == 2:
            ops.append(("ldx", 2, 4))
        ld(i)
    b2 = [0, 0]
    for i in range(n + 1):
        last = i >= n - 1
        y_ready = len(y_wait)
        hold[0] = not last
        if i >= 3 and b2[0] < E and (i % 2 == 1 or i == n - 2):
            ops.append(("b2s", b2[0]))
            b2[0] += 1
        if i >= 2 and b2[1] < E and (i % 2 == 0 or i == n - 3):
            ops.append(("b2p", b2[1]))
            b2[1] += 1
        if i in (1, 5, 9):
            ops.append(("xtp", i // 2 + 2, i // 2 + 4))
        if i == 0:
            cp("V", 0, 0, 0, 256)
            cp("S", 0, 0, 256, 512)
            cp("V", 0, 1)
            cp("S", 0, 2)
            ops.append(("consts",))
            ops.append(("exp",))
            ops.append(("xtp", 0, 2))
            q(0, 0, 2, False)
            cp("V", 0, 3)
            ops.append(("xcp", 0, 2))
        elif i < n:
            if i in V_MORE:
                cp("S", i, 2, 256, 512)
            else:
                cp("S", i, 2)
            cp("V", i, 0)
            cp("V", i, 1)
            if i in V_MORE:
                cp("V", i, 2, 0, 256)
            cp("S", i, 3)
        if i < n:
            if i in (1, 5):
                ops.append(("ldx", (i + 7) // 2, (i + 7) // 2 + 2))
            if i + AHEAD < n:
                ld(i + AHEAD)
        if i == 0:
            ops.append(("b1T",))
            ops.append(("xq", 0, 2))
            for c in (0, 1):
                ops.append(("mm1", 0, c))
                z_wait.append((0, c))
        if i in (2, 6, 10):
            ops.append(("xcp", i // 2 + 1, i // 2 + 3))
        if i > 1:
            if i == n:
                q(i - 1, 2, 3)
                q(i - 1, 3, 4)
            else:
                q(i - 1, 2, 4)
        hreg_slot(i)
        z_slot()
        hold[0] = False
        try_mm2()
        hold[0] = not last
        if i in (3, 7, 11):
            ops.append(("xq", (i + 1) // 2, (i + 1) // 2 + 2))
        if i == 0:
            q(0, 2, 4)
        elif i < n:
            q(i, 0, 2)
        hq_slot()
        if i + 1 in PE_HALF:
            ops.append(("pe", i + 1))
        y_slot(y_ready)
    hold[0] = False
    hreg_slot(n)
    hq_slot()
    y_slot(len(y_wait))
    return seq, ops


def tile_moelayer_kernel(tc, x, W1, b1, W2, b2, temperature, out):
    nc = tc.nc
    seq, ops = make_plan()
    with ExitStack() as ctx:
        const = ctx.enter_context(tc.tile_pool(name="const", bufs=1))
        rawp = ctx.enter_context(tc.tile_pool(name="raw", bufs=5))
        rawq = ctx.enter_context(tc.tile_pool(name="rawq", bufs=12))
        gp = ctx.enter_context(tc.tile_pool(name="gp", bufs=4))
        codes = ctx.enter_context(tc.tile_pool(name="codes", bufs=2))
        hp = ctx.enter_context(tc.tile_pool(name="hp", bufs=2))
        outp = ctx.enter_context(tc.tile_pool(name="outp", bufs=3))
        b2sp = ctx.enter_context(tc.tile_pool(name="b2sp", bufs=2))
        zp = ctx.enter_context(tc.psum_pool(name="zp", bufs=6))
        yp = ctx.enter_context(tc.psum_pool(name="yp", bufs=2))
        ctx.enter_context(tc.manual_schedule())

        raw = {}
        grouped = {}
        wc = {}
        ws = {}
        zt = {}
        hT = {}
        hg = {}
        hc = {}
        hs = {}
        yt = {}
        ot = {}
        held = {}
        pb = {}
        bs = {}
        pt = {}

        x_sb = const.tile([P, E, D], BF16, name="x_sb")
        xg = const.tile([P, E * P * 4], BF16, name="xg", align_bytes=64)
        xc = const.tile([P, E * P], U32, name="xc", align_bytes=64)
        xs = const.tile([P, E * P], U8, name="xs", align_bytes=64)
        x_words = x_sb[:].bitcast(F32).rearrange("p e (v u) -> p e u v", u=2)
        xg_words = xg[:].bitcast(F32).rearrange("p (e r u) -> p e r u", e=E, u=2)
        x_view = x.rearrange("(e r) d -> r e d", e=E)
        t_sb = const.tile([P, 1], BF16, name="t_sb")
        t_min = const.tile([P, 1], F32, name="t_min")
        s_col = const.tile([P, 1], F32, name="s_col")
        b1_raw = const.tile([P, 512], BF16, name="b1_raw")
        b1_g = const.tile([P, 4, P], BF16, name="b1_g")
        b1T = const.tile([P, 4, 32], F32, name="b1T")
        warm = const.tile([P, 2], F32, name="warm")
        b2_raw = const.tile([P, P], BF16, name="b2_raw")
        b2T = const.tile([P, 32], F32, name="b2T")
        ident_f = const.tile([P, P], F32, name="ident_f")
        ident_b = const.tile([P, P], BF16, name="ident_b")

        for op in ops:
            kind = op[0]
            if kind == "ldsmall":
                nc.vector.memset(warm[:], 0.0)
                nc.vector.memset(b1_raw[:], 0.0)
                nc.vector.memset(b2_raw[:], 0.0)
                nc.scalar.dma_start(out=t_sb[:], in_=temperature.partition_broadcast(P))
                nc.scalar.dma_start(out=b1_raw[0:32, :], in_=b1.rearrange("e (g f) -> (e g) f", g=4))
                nc.scalar.dma_start(out=b2_raw[0:32, :], in_=b2.rearrange("e (q f) -> (e q) f", q=4))
                nc.scalar.activation(out=warm[:, 1:2], in_=warm[:, 0:1], func=ACT.Exp)
                make_identity(nc, ident_f[:])
                make_identity(nc, ident_b[:])
            elif kind == "ld":
                i, a, b = op[1], op[2], op[3]
                mk, e = seq[i]
                n = b - a
                if n < 1024:
                    piece = rawq.tile([P, 4 * n], BF16, name="raw_%d_%d" % (i, a), tag="rawq")
                else:
                    piece = rawp.tile([P, 4 * n], BF16, name="raw_%d_%d" % (i, a), tag="raw")
                if mk == "W1":
                    src = W1[e].rearrange("(p j) w -> p j w", j=4)
                    rows = piece[:].rearrange("p (j w) -> p j w", j=4)
                    nc.sync.dma_start(out=rows, in_=src[:, :, a:b])
                    for lo in range(a, b, 256):
                        raw[(i, lo)] = (rows, lo - a)
                else:
                    src = W2[e].rearrange("(g p t) d -> p g (t d)", p=P, t=4)
                    rows = piece[:].rearrange("p (g w) -> p g w", g=n // 512)
                    nc.sync.dma_start(out=rows, in_=src[:, a // 512:b // 512, :])
                    for lo in range(a, b, 256):
                        raw[(i, lo)] = (rows[:, (lo - a) // 512, :].rearrange("p (t d) -> p t d", t=4), lo % 512)
            elif kind == "ldx":
                a, b = op[1], op[2]
                nc.sync.dma_start(out=x_sb[:, a:b, :], in_=x_view[:, a:b, :])
            elif kind == "consts":
                nc.vector.tensor_scalar_min(out=t_min[:], in0=t_sb[:], scalar1=CLAMP_MAX)
                nc.vector.tensor_copy(out=b1_g[:], in_=b1_raw[:].rearrange("p (m t) -> p t m", t=4))
                b1_ps = zp.tile([P, 5, P], BF16, name="b1_ps", tag="z")
                for t in range(4):
                    nc.tensor.transpose(b1_ps[:, t, :], b1_g[:, t, :], ident_b[:])
                nc.tensor.transpose(b1_ps[:, 4, :], b2_raw[:], ident_b[:])
                held["b1_ps"] = b1_ps
            elif kind == "b1T":
                nc.vector.tensor_copy(out=b1T[:], in_=held["b1_ps"][:, 0:4, 0:32])
                nc.vector.tensor_scalar_mul(out=b2T[:], in0=held["b1_ps"][:, 4, 0:32], scalar1=s_col[:, 0:1])
            elif kind == "exp":
                nc.scalar.activation(out=s_col[:], in_=t_min[:], func=ACT.Exp)
            elif kind == "xtp":
                pair = op[1] // 2
                xt = zp.tile([P, 4, P], F32, name="xt", tag="z")
                held[("xt", pair)] = xt
                for a in range(2):
                    for u in range(2):
                        nc.tensor.transpose(xt[:, 2 * a + u, :], x_words[:, 2 * pair + a, u, :], ident_f[:])
            elif kind == "xcp":
                pair = op[1] // 2
                nc.scalar.copy(out=xg_words[:, 2 * pair:2 * pair + 2, :, :],
                               in_=held[("xt", pair)][:].rearrange("p (a u) r -> p a r u", u=2))
            elif kind == "xq":
                a, b = op[1], op[2]
                nc.vector.quantize_mx(out=xc[:, P * a:P * b].bitcast(FP8X4), scales=xs[:, P * a:P * b],
                                      in_=xg[:, 4 * P * a:4 * P * b])
            elif kind == "pe":
                i = op[1]
                mk, e = seq[i]
                rows, first = raw[(i, 1792)]
                pt[i] = zp.tile([P, 1024], BF16, name="pt", tag="z")
                for part in range(2):
                    lo = first + P * part
                    if mk == "W1":
                        src = rows[:, :, lo:lo + P].rearrange("p j (m t) -> p j m t", t=4)
                        dst = pt[i][:].rearrange("p (t m j) -> p j m t", t=4, j=4)[:, :, 32 * part:32 * part + 32]
                    else:
                        src = rows[:, :, lo:lo + P]
                        dst = pt[i][:].rearrange("p (d t) -> p t d", t=4)[:, :, P * part:P * part + P]
                    nc.tensor.matmul(out=dst, lhsT=ident_b[:], rhs=src, start=True, stop=True)
            elif kind == "cp":
                eng, i, c, lo, hi = op[1:]
                mk, e = seq[i]
                if (i, c // 2) not in grouped:
                    grouped[(i, c // 2)] = gp.tile([P, 4096], BF16, name="g", align_bytes=64)
                g = grouped[(i, c // 2)][:, 2048 * (c % 2):2048 * (c % 2) + 2048]
                if eng == "PE":
                    if mk == "W1":
                        nc.scalar.copy(out=g.rearrange("p (t w) -> p t w", t=4)[:, :, 256:512],
                                       in_=pt[i][:].rearrange("p (t w) -> p t w", t=4))
                    else:
                        nc.scalar.copy(out=g[:, 1024:2048], in_=pt[i][:])
                else:
                    rows, first = raw[(i, 512 * c + lo)]
                    part = rows[:, :, first:first + hi - lo]
                    if mk == "W1" and eng == "V":
                        dst = g.rearrange("p (h l m u j) -> p h m j u l", h=2, l=2, u=2, j=4)[:, :, lo // 8:hi // 8]
                        src = part.rearrange("p j (m u h l) -> p h m j u l", u=2, h=2, l=2)
                        for h in range(2):
                            nc.vector.tensor_copy(out=dst[:, h], in_=src[:, h])
                        continue
                    if mk == "W1":
                        dst = g.rearrange("p (t m u j) -> p m j u t", t=4, u=2, j=4)[:, lo // 8:hi // 8]
                        src = part.rearrange("p j (m u t) -> p m j u t", u=2, t=4)
                    else:
                        run = 2 if eng == "V" else 4
                        dst = g.rearrange("p (c i t) -> p c t i", i=run, t=4)[:, lo // run:hi // run]
                        src = part.rearrange("p t (c i) -> p c t i", i=run)
                    if eng == "V":
                        nc.vector.tensor_copy(out=dst, in_=src)
                    else:
                        nc.scalar.copy(out=dst, in_=src)
            elif kind == "q":
                i, c0, c1 = op[1:]
                mk, e = seq[i]
                if i not in wc:
                    wc[i] = codes.tile([P, 2048], U32, name="c_%d" % i, tag="c" + mk, align_bytes=64)
                    ws[i] = codes.tile([P, 2048], U8, name="s_%d" % i, tag="s" + mk, align_bytes=64)
                first = 2048 * (c0 % 2)
                nc.vector.quantize_mx(out=wc[i][:, 512 * c0:512 * c1].bitcast(FP8X4),
                                      scales=ws[i][:, 512 * c0:512 * c1],
                                      in_=grouped[(i, c0 // 2)][:, first:first + 2048 * (c1 - c0)])
            elif kind == "mm1":
                e, g = op[1], op[2]
                i = seq.index(("W1", e))
                z = zp.tile([P, 4, P], F32, name="z", tag="z")
                zt[(e, g)] = z
                for t in range(4):
                    lo = 512 * g + P * t
                    nc.tensor.matmul_mx(out=z[:, t, :],
                                        lhsT=wc[i][:, lo:lo + P].bitcast(FP8X4), lhsT_scale=ws[i][:, lo:lo + P],
                                        rhs=xc[:, P * e:P * e + P].bitcast(FP8X4), rhs_scale=xs[:, P * e:P * e + P],
                                        start=True, stop=True)
            elif kind == "zout":
                e, g = op[1], op[2]
                if e not in hT:
                    hT[e] = hp.tile([P, 4, 512], BF16, name="hT")
                for t in range(4):
                    nc.scalar.activation(out=hT[e][:, t, P * g:P * g + P], in_=zt[(e, g)][:, t, :], func=ACT.Relu,
                                         bias=b1T[:, t, 4 * e + g:4 * e + g + 1], scale=1.0)
            elif kind == "hreg":
                e = op[1]
                hg[e] = hp.tile([P, 2048], BF16, name="hg", align_bytes=64)
                nc.vector.tensor_copy(out=hg[e][:].rearrange("p (c i t) -> p c t i", i=2, t=4),
                                      in_=hT[e][:].rearrange("p t (c i) -> p c t i", i=2))
            elif kind == "hq":
                e = op[1]
                hc[e] = hp.tile([P, 512], U32, name="hc", align_bytes=64)
                hs[e] = hp.tile([P, 512], U8, name="hs", align_bytes=64)
                nc.vector.quantize_mx(out=hc[e][:].bitcast(FP8X4), scales=hs[e][:], in_=hg[e][:])
            elif kind == "mm2":
                e, c, first, last = op[1], op[2], op[3], op[4]
                i = seq.index(("W2", e))
                if first:
                    yt[e] = yp.tile([P, D], F32, name="y")
                nc.tensor.matmul_mx(out=yt[e][:],
                                    lhsT=hc[e][:, P * c:P * c + P].bitcast(FP8X4), lhsT_scale=hs[e][:, P * c:P * c + P],
                                    rhs=wc[i][:, 512 * c:512 * c + 512].bitcast(FP8X4),
                                    rhs_scale=ws[i][:, 512 * c:512 * c + 512],
                                    start=first, stop=last)
            elif kind == "b2s":
                e = op[1]
                bs[e] = b2sp.tile([P, D], F32, name="bs")
                nc.scalar.copy(out=bs[e][:], in_=pb[e][:].rearrange("p a b -> p (a b)"))
            elif kind == "b2p":
                e = op[1]
                pb[e] = zp.tile([P, 4, P], F32, name="pb", tag="z")
                for q4 in range(4):
                    nc.tensor.transpose(pb[e][:, q4, :], b2T[:, 4 * e + q4:4 * e + q4 + 1].to_broadcast([P, P]), ident_f[:])
            elif kind == "yout":
                e = op[1]
                ot[e] = outp.tile([P, D], F32, name="o_sb")
                nc.vector.scalar_tensor_tensor(out=ot[e][:], in0=yt[e][:], scalar=s_col[:, 0:1],
                                               in1=bs[e][:], op0=ALU.mult, op1=ALU.add)
            elif kind == "st":
                e = op[1]
                nc.sync.dma_start(out=out[P * e:P * e + P, :], in_=ot[e][:])
